import numpy as np
import ml_dtypes


def mxq(x, axis, fmt="e4m3"):
    dtype, down = {"e4m3": (ml_dtypes.float8_e4m3fn, 7), "e5m2": (ml_dtypes.float8_e5m2, 14)}[fmt]
    v = np.moveaxis(np.asarray(x, np.float32).astype(ml_dtypes.bfloat16).astype(np.float64), axis, -1)
    blocks = v.reshape(v.shape[:-1] + (-1, 32))
    amax = np.abs(blocks).max(-1, keepdims=True)
    byte = np.maximum(np.where(amax > 0, np.frexp(amax)[1] - 1 + 127, 0) - down, 1)
    scale = np.exp2(byte - 127.0)
    codes = (blocks / scale).astype(np.float32).astype(dtype).astype(np.float64)
    return np.moveaxis((codes * scale).reshape(v.shape), -1, axis)


WIDE = False


def mx_kscale(k):
    if not WIDE:
        return np.ones(k)
    levels = np.array([10, -10, 5, -5, 0])
    if k % 512:
        return np.exp2(np.random.permutation(np.resize(levels, k // 32))).repeat(32)
    a = np.empty((k // 512, 16))
    for p in range(k // 512):
        a[p, :8] = np.random.permutation(np.resize(levels, 8))
        for g in range(8):
            far = levels[np.abs(levels - a[p, g]) >= 10]
            a[p, g + 8] = far[np.random.randint(len(far))]
    return np.exp2(a.ravel()).repeat(32)


BF16 = ml_dtypes.bfloat16


def bf(x):
    return np.asarray(x, np.float32).astype(BF16)


def f64(x):
    return np.asarray(x).astype(np.float64)


B, C, Q, O, H, W = 2, 2560, 512, 512, 16, 32
N = H * W
SIG = 1.75


def setup_inputs():
    s = mx_kscale(N).reshape(H, W)
    return {"x": bf(np.random.standard_normal((B, C, H, W)) / s),
            "query": bf(np.random.standard_normal((B, Q, H, W)) * SIG / np.sqrt(N) * s)}


def core(x, query):
    xf = f64(x).reshape(B, C, N)
    qf = f64(query).reshape(B, Q, N)
    energy = mxq(qf, 2, "e4m3") @ mxq(xf, 2, "e4m3").transpose(0, 2, 1)
    energy_new = energy.max(-1, keepdims=True) - energy
    e = np.exp(energy_new - energy_new.max(-1, keepdims=True))
    return e / e.sum(-1, keepdims=True)


def e4m3fn_bytes(y):
    return np.clip(np.asarray(y, np.float64), -448.0, 448.0).astype(np.float32).astype(ml_dtypes.float8_e4m3fn).view(np.uint8)


Y_SCALE = 250000.0


def reference(x, query):
    out = core(x, query)
    return out, e4m3fn_bytes(out * Y_SCALE)

@@ -1,0 +1,162 @@
+from contextlib import ExitStack
+
+import concourse.mybir as mybir
+from concourse.masks import make_identity
+
+B, C, Q, K = 2, 2560, 512, 512
+FLOPS = 2 * B * Q * C * K
+Y_SCALE = 250000.0
+
+F32 = mybir.dt.float32
+BF16 = mybir.dt.bfloat16
+U32 = mybir.dt.uint32
+U8 = mybir.dt.uint8
+FP8X4 = mybir.dt.float8_e4m3fn_x4
+FP8 = mybir.dt.float8_e4m3fn
+ALU = mybir.AluOpType
+ACT = mybir.ActivationFunctionType
+AX = mybir.AxisListType
+
+P = 128
+CH = 512
+NJ = C // CH
+NM = Q // P
+WARM = 6
+HALF = C // 2
+LAG = 3
+
+
+def tile_guided_cam_module_pa_kernel(tc, x, query, out_0, out_1):
+    nc = tc.nc
+    xf = x.rearrange("b c y w -> b c (y w)")
+    qf = query.rearrange("b c y w -> b c (y w)")
+
+    with ExitStack() as ctx:
+        const = ctx.enter_context(tc.tile_pool(name="const", bufs=1))
+        rawp = ctx.enter_context(tc.tile_pool(name="rawp", bufs=12))
+        grpp = ctx.enter_context(tc.tile_pool(name="grpp", bufs=4))
+        codp = ctx.enter_context(tc.tile_pool(name="codp", bufs=12))
+        wp = ctx.enter_context(tc.tile_pool(name="wp", bufs=8))
+        f8p = ctx.enter_context(tc.tile_pool(name="f8p", bufs=8))
+        scp = ctx.enter_context(tc.tile_pool(name="scp", bufs=2))
+        stp = ctx.enter_context(tc.tile_pool(name="stp", bufs=8))
+        tpp = ctx.enter_context(tc.psum_pool(name="tpp", bufs=3))
+        mxp = ctx.enter_context(tc.psum_pool(name="mxp", bufs=5))
+
+        chunks = []
+        for b in range(B):
+            chunks.append(qf[b, :, :])
+            for j in range(NJ):
+                chunks.append(xf[b, j * CH:(j + 1) * CH, :])
+        raws = []
+        for c in range(len(chunks)):
+            raw = rawp.tile([P, 2, 2 * K], BF16)
+            nc.sync.dma_start(out=raw[:], in_=chunks[c].rearrange("(h r i) k -> r h (i k)", h=2, i=2))
+            raws.append(raw)
+
+        ident = const.tile([P, P], F32)
+        make_identity(nc, ident[:])
+        warm = const.tile([P, CH], BF16)
+        nc.vector.memset(warm[:], 0.0)
+        zero = const.tile([P, 1], F32)
+        nc.vector.memset(zero[:], 0.0)
+        junk = const.tile([P, 1], F32)
+        nc.scalar.activation(out=junk[:], in_=zero[:], func=ACT.Exp)
+        wps = mxp.tile([P, CH], F32, name="acc")
+        for d in range(WARM):
+            nc.tensor.matmul(out=wps[:], lhsT=warm[:, 0:P], rhs=warm[:], start=True, stop=True)
+
+        codes = {}
+        scales = {}
+
+        def prep(c, engines):
+            grp = grpp.tile([P, 4 * CH], BF16, align_bytes=64)
+            g32 = grp[:].bitcast(F32)
+            for h in range(2):
+                words = raws[c][:, h, :].bitcast(F32)
+                tp = tpp.tile([P, 4 * P], F32)
+                for s in range(4):
+                    i, u = s // 2, s % 2
+                    nc.tensor.transpose(tp[:, s * P:(s + 1) * P], words[:, 256 * i + u:256 * (i + 1):2], ident[:])
+                dst = g32[:, 512 * h:512 * (h + 1)].rearrange("p (r s) -> p r s", s=4)
+                src = tp[:].rearrange("p (s r) -> p r s", s=4)
+                if engines[h] == "s":
+                    nc.scalar.copy(out=dst, in_=src)
+                else:
+                    nc.vector.tensor_copy(out=dst, in_=src)
+            cod = codp.tile([P, CH], U32, align_bytes=64)
+            scl = codp.tile([P, CH], U8, align_bytes=64)
+            nc.vector.quantize_mx(out=cod[:].bitcast(FP8X4), scales=scl[:], in_=grp[:])
+            codes[c] = cod
+            scales[c] = scl
+
+        wt = {}
+        mins = {}
+
+        def unit(t, j):
+            b, m = t // NM, t % NM
+            cq = b * (NJ + 1)
+            cx = cq + 1 + j
+            if j == 0:
+                w_new = wp.tile([P, C], F32, name="w")
+                mn_new = stp.tile([P, 8], F32, name="mn")
+                wt[t] = w_new
+                mins[t] = mn_new
+            acc = mxp.tile([P, CH], F32, name="acc")
+            nc.tensor.matmul_mx(
+                out=acc[:],
+                lhsT=codes[cq][:, m * P:(m + 1) * P].bitcast(FP8X4),
+                lhsT_scale=scales[cq][:, m * P:(m + 1) * P],
+                rhs=codes[cx][:].bitcast(FP8X4),
+                rhs_scale=scales[cx][:],
+                start=True,
+                stop=True,
+            )
+            nc.vector.tensor_scalar(
+                out=wt[t][:, j * CH:(j + 1) * CH], in0=acc[:], scalar1=1.0, scalar2=None,
+                op0=ALU.mult, op1=ALU.min, accum_out=mins[t][:, j:j + 1],
+            )
+
+        def soft(t):
+            b, m = t // NM, t % NM
+            w = wt[t]
+            rmin = stp.tile([P, 1], F32, name="rmin")
+            nc.vector.tensor_reduce(out=rmin[:], in_=mins[t][:, 0:NJ], axis=AX.X, op=ALU.min)
+            rsum = stp.tile([P, 1], F32, name="rsum")
+            nc.scalar.activation(out=w[:], in_=w[:], func=ACT.Exp, bias=rmin[:], scale=-1.0, accum_out=rsum[:])
+            rinv = stp.tile([P, 1], F32, name="rinv")
+            nc.vector.reciprocal(out=rinv[:], in_=rsum[:])
+            for a in (0, HALF):
+                nc.gpsimd.tensor_scalar(out=w[:, a:a + HALF], in0=w[:, a:a + HALF], scalar1=rinv[:], scalar2=0.0, op0=ALU.mult, op1=ALU.add)
+                nc.sync.dma_start(out=out_0[b, m * P:(m + 1) * P, a:a + HALF], in_=w[:, a:a + HALF])
+
+        def cast(t):
+            b, m = t // NM, t % NM
+            w = wt[t]
+            f8 = f8p.tile([P, C], FP8, name="f8")
+            sc = scp.tile([P, HALF], F32, name="sc")
+            nc.vector.tensor_scalar(out=sc[:], in0=w[:, 0:HALF], scalar1=Y_SCALE, scalar2=None, op0=ALU.mult)
+            nc.vector.tensor_copy(out=f8[:, 0:HALF], in_=sc[:], saturate=False)
+            nc.scalar.activation(out=f8[:, HALF:C], in_=w[:, HALF:C], func=ACT.Copy, scale=Y_SCALE, saturate=False)
+            nc.sync.dma_start(out=out_1[b, m * P:(m + 1) * P, :], in_=f8[:].bitcast(U8))
+
+        prep(0, "ss")
+        prep(1, "ss")
+        for j in range(NJ):
+            if j + 1 < NJ:
+                prep(2 + j, "ss")
+            unit(0, j)
+        soft(0)
+        nxt = NJ + 1
+        for t in range(1, B * NM):
+            if t < NM:
+                prep(nxt, "ss")
+                prep(nxt + 1, "ss")
+                nxt += 2
+            for j in range(NJ):
+                unit(t, j)
+            soft(t)
+            if t >= LAG:
+                cast(t - LAG)
+        for t in range(B * NM - LAG, B * NM):
+            cast(t)

@@ -23,7 +23,8 @@ NJ = C // CH
 NM = Q // P
 WARM = 6
 HALF = C // 2
-LAG = 3
+VC = 640
+LAG = 2
 
 
 def tile_guided_cam_module_pa_kernel(tc, x, query, out_0, out_1):
@@ -127,17 +128,17 @@ def tile_guided_cam_module_pa_kernel(tc, x, query, out_0, out_1):
             rinv = stp.tile([P, 1], F32, name="rinv")
             nc.vector.reciprocal(out=rinv[:], in_=rsum[:])
             for a in (0, HALF):
-                nc.gpsimd.tensor_scalar(out=w[:, a:a + HALF], in0=w[:, a:a + HALF], scalar1=rinv[:], scalar2=0.0, op0=ALU.mult, op1=ALU.add)
+                nc.vector.tensor_scalar(out=w[:, a:a + HALF], in0=w[:, a:a + HALF], scalar1=rinv[:], scalar2=None, op0=ALU.mult)
                 nc.sync.dma_start(out=out_0[b, m * P:(m + 1) * P, a:a + HALF], in_=w[:, a:a + HALF])
 
         def cast(t):
             b, m = t // NM, t % NM
             w = wt[t]
             f8 = f8p.tile([P, C], FP8, name="f8")
-            sc = scp.tile([P, HALF], F32, name="sc")
-            nc.vector.tensor_scalar(out=sc[:], in0=w[:, 0:HALF], scalar1=Y_SCALE, scalar2=None, op0=ALU.mult)
-            nc.vector.tensor_copy(out=f8[:, 0:HALF], in_=sc[:], saturate=False)
-            nc.scalar.activation(out=f8[:, HALF:C], in_=w[:, HALF:C], func=ACT.Copy, scale=Y_SCALE, saturate=False)
+            sc = scp.tile([P, VC], F32, name="sc")
+            nc.vector.tensor_scalar(out=sc[:], in0=w[:, 0:VC], scalar1=Y_SCALE, scalar2=None, op0=ALU.mult)
+            nc.vector.tensor_copy(out=f8[:, 0:VC], in_=sc[:], saturate=False)
+            nc.scalar.activation(out=f8[:, VC:C], in_=w[:, VC:C], func=ACT.Copy, scale=Y_SCALE, saturate=False)
             nc.sync.dma_start(out=out_1[b, m * P:(m + 1) * P, :], in_=f8[:].bitcast(U8))
 
         prep(0, "ss")

@@ -23,8 +23,8 @@ NJ = C // CH
 NM = Q // P
 WARM = 6
 HALF = C // 2
-VC = 640
-LAG = 2
+G_NORM = 6
+S_CAST = 4
 
 
 def tile_guided_cam_module_pa_kernel(tc, x, query, out_0, out_1):
@@ -52,7 +52,11 @@ def tile_guided_cam_module_pa_kernel(tc, x, query, out_0, out_1):
         raws = []
         for c in range(len(chunks)):
             raw = rawp.tile([P, 2, 2 * K], BF16)
-            nc.sync.dma_start(out=raw[:], in_=chunks[c].rearrange("(h r i) k -> r h (i k)", h=2, i=2))
+            if c < 2:
+                for h in range(2):
+                    nc.sync.dma_start(out=raw[:, h, :], in_=chunks[c][h * 2 * P:(h + 1) * 2 * P, :].rearrange("(r i) k -> r (i k)", i=2))
+            else:
+                nc.sync.dma_start(out=raw[:], in_=chunks[c].rearrange("(h r i) k -> r h (i k)", h=2, i=2))
             raws.append(raw)
 
         ident = const.tile([P, P], F32)
@@ -128,17 +132,27 @@ def tile_guided_cam_module_pa_kernel(tc, x, query, out_0, out_1):
             rinv = stp.tile([P, 1], F32, name="rinv")
             nc.vector.reciprocal(out=rinv[:], in_=rsum[:])
             for a in (0, HALF):
-                nc.vector.tensor_scalar(out=w[:, a:a + HALF], in0=w[:, a:a + HALF], scalar1=rinv[:], scalar2=None, op0=ALU.mult)
+                if t < G_NORM:
+                    nc.gpsimd.tensor_scalar(out=w[:, a:a + HALF], in0=w[:, a:a + HALF], scalar1=rinv[:], scalar2=0.0, op0=ALU.mult, op1=ALU.add)
+                else:
+                    nc.vector.tensor_scalar(out=w[:, a:a + HALF], in0=w[:, a:a + HALF], scalar1=rinv[:], scalar2=None, op0=ALU.mult)
                 nc.sync.dma_start(out=out_0[b, m * P:(m + 1) * P, a:a + HALF], in_=w[:, a:a + HALF])
 
         def cast(t):
             b, m = t // NM, t % NM
             w = wt[t]
             f8 = f8p.tile([P, C], FP8, name="f8")
-            sc = scp.tile([P, VC], F32, name="sc")
-            nc.vector.tensor_scalar(out=sc[:], in0=w[:, 0:VC], scalar1=Y_SCALE, scalar2=None, op0=ALU.mult)
-            nc.vector.tensor_copy(out=f8[:, 0:VC], in_=sc[:], saturate=False)
-            nc.scalar.activation(out=f8[:, VC:C], in_=w[:, VC:C], func=ACT.Copy, scale=Y_SCALE, saturate=False)
+            if t < S_CAST:
+                for a in (0, HALF):
+                    nc.scalar.activation(out=f8[:, a:a + HALF], in_=w[:, a:a + HALF], func=ACT.Copy, scale=Y_SCALE, saturate=False)
+            else:
+                scs = []
+                for a in (0, HALF):
+                    sc = scp.tile([P, HALF], F32, name="sc")
+                    nc.vector.tensor_scalar(out=sc[:], in0=w[:, a:a + HALF], scalar1=Y_SCALE, scalar2=None, op0=ALU.mult)
+                    scs.append(sc)
+                for a in (0, HALF):
+                    nc.vector.tensor_copy(out=f8[:, a:a + HALF], in_=scs[a // HALF][:], saturate=False)
             nc.sync.dma_start(out=out_1[b, m * P:(m + 1) * P, :], in_=f8[:].bitcast(U8))
 
         prep(0, "ss")
@@ -157,7 +171,5 @@ def tile_guided_cam_module_pa_kernel(tc, x, query, out_0, out_1):
             for j in range(NJ):
                 unit(t, j)
             soft(t)
-            if t >= LAG:
-                cast(t - LAG)
-        for t in range(B * NM - LAG, B * NM):
+        for t in range(B * NM):
             cast(t)

@@ -24,7 +24,7 @@ NM = Q // P
 WARM = 6
 HALF = C // 2
 G_NORM = 6
-S_CAST = 4
+S_CAST = 6
 
 
 def tile_guided_cam_module_pa_kernel(tc, x, query, out_0, out_1):

@@ -24,7 +24,8 @@ NM = Q // P
 WARM = 6
 HALF = C // 2
 G_NORM = 6
-S_CAST = 6
+S_CAST = 1
+QUART = C // 4
 
 
 def tile_guided_cam_module_pa_kernel(tc, x, query, out_0, out_1):
@@ -142,17 +143,17 @@ def tile_guided_cam_module_pa_kernel(tc, x, query, out_0, out_1):
             b, m = t // NM, t % NM
             w = wt[t]
             f8 = f8p.tile([P, C], FP8, name="f8")
-            if t < S_CAST:
-                for a in (0, HALF):
-                    nc.scalar.activation(out=f8[:, a:a + HALF], in_=w[:, a:a + HALF], func=ACT.Copy, scale=Y_SCALE, saturate=False)
-            else:
+            s_from = 0 if t < S_CAST else HALF
+            if s_from > 0:
                 scs = []
-                for a in (0, HALF):
-                    sc = scp.tile([P, HALF], F32, name="sc")
-                    nc.vector.tensor_scalar(out=sc[:], in0=w[:, a:a + HALF], scalar1=Y_SCALE, scalar2=None, op0=ALU.mult)
+                for a in (0, QUART):
+                    sc = scp.tile([P, QUART], F32, name="sc")
+                    nc.vector.tensor_scalar(out=sc[:], in0=w[:, a:a + QUART], scalar1=Y_SCALE, scalar2=None, op0=ALU.mult)
                     scs.append(sc)
-                for a in (0, HALF):
-                    nc.vector.tensor_copy(out=f8[:, a:a + HALF], in_=scs[a // HALF][:], saturate=False)
+                for a in (0, QUART):
+                    nc.vector.tensor_copy(out=f8[:, a:a + QUART], in_=scs[a // QUART][:], saturate=False)
+            for a in range(s_from, C, QUART):
+                nc.scalar.activation(out=f8[:, a:a + QUART], in_=w[:, a:a + QUART], func=ACT.Copy, scale=Y_SCALE, saturate=False)
             nc.sync.dma_start(out=out_1[b, m * P:(m + 1) * P, :], in_=f8[:].bitcast(U8))
 
         prep(0, "ss")
@@ -162,12 +163,9 @@ def tile_guided_cam_module_pa_kernel(tc, x, query, out_0, out_1):
                 prep(2 + j, "ss")
             unit(0, j)
         soft(0)
-        nxt = NJ + 1
+        for c in range(NJ + 1, 2 * (NJ + 1)):
+            prep(c, "ss")
         for t in range(1, B * NM):
-            if t < NM:
-                prep(nxt, "ss")
-                prep(nxt + 1, "ss")
-                nxt += 2
             for j in range(NJ):
                 unit(t, j)
             soft(t)

from contextlib import ExitStack

import concourse.mybir as mybir
from concourse.masks import make_identity

B, C, Q, K = 2, 2560, 512, 512
FLOPS = 2 * B * Q * C * K
Y_SCALE = 250000.0

F32 = mybir.dt.float32
BF16 = mybir.dt.bfloat16
U32 = mybir.dt.uint32
U8 = mybir.dt.uint8
FP8X4 = mybir.dt.float8_e4m3fn_x4
FP8 = mybir.dt.float8_e4m3fn
ALU = mybir.AluOpType
ACT = mybir.ActivationFunctionType
AX = mybir.AxisListType

P = 128
CH = 512
NJ = C // CH
NM = Q // P
WARM = 6
HALF = C // 2
G_NORM = 6
S_CAST = 1
QUART = C // 4


def tile_guided_cam_module_pa_kernel(tc, x, query, out_0, out_1):
    nc = tc.nc
    xf = x.rearrange("b c y w -> b c (y w)")
    qf = query.rearrange("b c y w -> b c (y w)")

    with ExitStack() as ctx:
        const = ctx.enter_context(tc.tile_pool(name="const", bufs=1))
        rawp = ctx.enter_context(tc.tile_pool(name="rawp", bufs=12))
        grpp = ctx.enter_context(tc.tile_pool(name="grpp", bufs=4))
        codp = ctx.enter_context(tc.tile_pool(name="codp", bufs=12))
        wp = ctx.enter_context(tc.tile_pool(name="wp", bufs=8))
        f8p = ctx.enter_context(tc.tile_pool(name="f8p", bufs=8))
        scp = ctx.enter_context(tc.tile_pool(name="scp", bufs=2))
        stp = ctx.enter_context(tc.tile_pool(name="stp", bufs=8))
        tpp = ctx.enter_context(tc.psum_pool(name="tpp", bufs=3))
        mxp = ctx.enter_context(tc.psum_pool(name="mxp", bufs=5))

        chunks = []
        for b in range(B):
            chunks.append(qf[b, :, :])
            for j in range(NJ):
                chunks.append(xf[b, j * CH:(j + 1) * CH, :])
        raws = []
        for c in range(len(chunks)):
            raw = rawp.tile([P, 2, 2 * K], BF16)
            if c < 2:
                for h in range(2):
                    nc.sync.dma_start(out=raw[:, h, :], in_=chunks[c][h * 2 * P:(h + 1) * 2 * P, :].rearrange("(r i) k -> r (i k)", i=2))
            else:
                nc.sync.dma_start(out=raw[:], in_=chunks[c].rearrange("(h r i) k -> r h (i k)", h=2, i=2))
            raws.append(raw)

        ident = const.tile([P, P], F32)
        make_identity(nc, ident[:])
        warm = const.tile([P, CH], BF16)
        nc.vector.memset(warm[:], 0.0)
        zero = const.tile([P, 1], F32)
        nc.vector.memset(zero[:], 0.0)
        junk = const.tile([P, 1], F32)
        nc.scalar.activation(out=junk[:], in_=zero[:], func=ACT.Exp)
        wps = mxp.tile([P, CH], F32, name="acc")
        for d in range(WARM):
            nc.tensor.matmul(out=wps[:], lhsT=warm[:, 0:P], rhs=warm[:], start=True, stop=True)

        codes = {}
        scales = {}

        def prep(c, engines):
            grp = grpp.tile([P, 4 * CH], BF16, align_bytes=64)
            g32 = grp[:].bitcast(F32)
            for h in range(2):
                words = raws[c][:, h, :].bitcast(F32)
                tp = tpp.tile([P, 4 * P], F32)
                for s in range(4):
                    i, u = s // 2, s % 2
                    nc.tensor.transpose(tp[:, s * P:(s + 1) * P], words[:, 256 * i + u:256 * (i + 1):2], ident[:])
                dst = g32[:, 512 * h:512 * (h + 1)].rearrange("p (r s) -> p r s", s=4)
                src = tp[:].rearrange("p (s r) -> p r s", s=4)
                if engines[h] == "s":
                    nc.scalar.copy(out=dst, in_=src)
                else:
                    nc.vector.tensor_copy(out=dst, in_=src)
            cod = codp.tile([P, CH], U32, align_bytes=64)
            scl = codp.tile([P, CH], U8, align_bytes=64)
            nc.vector.quantize_mx(out=cod[:].bitcast(FP8X4), scales=scl[:], in_=grp[:])
            codes[c] = cod
            scales[c] = scl

        wt = {}
        mins = {}

        def unit(t, j):
            b, m = t // NM, t % NM
            cq = b * (NJ + 1)
            cx = cq + 1 + j
            if j == 0:
                w_new = wp.tile([P, C], F32, name="w")
                mn_new = stp.tile([P, 8], F32, name="mn")
                wt[t] = w_new
                mins[t] = mn_new
            acc = mxp.tile([P, CH], F32, name="acc")
            nc.tensor.matmul_mx(
                out=acc[:],
                lhsT=codes[cq][:, m * P:(m + 1) * P].bitcast(FP8X4),
                lhsT_scale=scales[cq][:, m * P:(m + 1) * P],
                rhs=codes[cx][:].bitcast(FP8X4),
                rhs_scale=scales[cx][:],
                start=True,
                stop=True,
            )
            nc.vector.tensor_scalar(
                out=wt[t][:, j * CH:(j + 1) * CH], in0=acc[:], scalar1=1.0, scalar2=None,
                op0=ALU.mult, op1=ALU.min, accum_out=mins[t][:, j:j + 1],
            )

        def soft(t):
            b, m = t // NM, t % NM
            w = wt[t]
            rmin = stp.tile([P, 1], F32, name="rmin")
            nc.vector.tensor_reduce(out=rmin[:], in_=mins[t][:, 0:NJ], axis=AX.X, op=ALU.min)
            rsum = stp.tile([P, 1], F32, name="rsum")
            nc.scalar.activation(out=w[:], in_=w[:], func=ACT.Exp, bias=rmin[:], scale=-1.0, accum_out=rsum[:])
            rinv = stp.tile([P, 1], F32, name="rinv")
            nc.vector.reciprocal(out=rinv[:], in_=rsum[:])
            for a in (0, HALF):
                if t < G_NORM:
                    nc.gpsimd.tensor_scalar(out=w[:, a:a + HALF], in0=w[:, a:a + HALF], scalar1=rinv[:], scalar2=0.0, op0=ALU.mult, op1=ALU.add)
                else:
                    nc.vector.tensor_scalar(out=w[:, a:a + HALF], in0=w[:, a:a + HALF], scalar1=rinv[:], scalar2=None, op0=ALU.mult)
                nc.sync.dma_start(out=out_0[b, m * P:(m + 1) * P, a:a + HALF], in_=w[:, a:a + HALF])

        def cast(t):
            b, m = t // NM, t % NM
            w = wt[t]
            f8 = f8p.tile([P, C], FP8, name="f8")
            s_from = 0 if t < S_CAST else HALF
            if s_from > 0:
                scs = []
                for a in (0, QUART):
                    sc = scp.tile([P, QUART], F32, name="sc")
                    nc.vector.tensor_scalar(out=sc[:], in0=w[:, a:a + QUART], scalar1=Y_SCALE, scalar2=None, op0=ALU.mult)
                    scs.append(sc)
                for a in (0, QUART):
                    nc.vector.tensor_copy(out=f8[:, a:a + QUART], in_=scs[a // QUART][:], saturate=False)
            for a in range(s_from, C, QUART):
                nc.scalar.activation(out=f8[:, a:a + QUART], in_=w[:, a:a + QUART], func=ACT.Copy, scale=Y_SCALE, saturate=False)
            nc.sync.dma_start(out=out_1[b, m * P:(m + 1) * P, :], in_=f8[:].bitcast(U8))

        prep(0, "ss")
        prep(1, "ss")
        for j in range(NJ):
            if j + 1 < NJ:
                prep(2 + j, "ss")
            unit(0, j)
        soft(0)
        for c in range(NJ + 1, 2 * (NJ + 1)):
            prep(c, "ss")
        for t in range(1, B * NM):
            for j in range(NJ):
                unit(t, j)
            soft(t)
        for t in range(B * NM):
            cast(t)
